import numpy as np
import ml_dtypes


def mxq(x, axis, fmt="e4m3"):
    dtype, down = {"e4m3": (ml_dtypes.float8_e4m3fn, 7), "e5m2": (ml_dtypes.float8_e5m2, 14)}[fmt]
    v = np.moveaxis(np.asarray(x, np.float32).astype(ml_dtypes.bfloat16).astype(np.float64), axis, -1)
    blocks = v.reshape(v.shape[:-1] + (-1, 32))
    amax = np.abs(blocks).max(-1, keepdims=True)
    byte = np.maximum(np.where(amax > 0, np.frexp(amax)[1] - 1 + 127, 0) - down, 1)
    scale = np.exp2(byte - 127.0)
    codes = (blocks / scale).astype(np.float32).astype(dtype).astype(np.float64)
    return np.moveaxis((codes * scale).reshape(v.shape), -1, axis)


WIDE = False


def mx_kscale(k):
    if not WIDE:
        return np.ones(k)
    levels = np.array([10, -10, 5, -5, 0])
    a = np.random.permutation(np.resize(levels, k // 512 * 4)).reshape(k // 512, 4)
    idx = np.arange(k)
    return np.exp2(a[idx // 512, idx % 128 // 32])


BF16 = ml_dtypes.bfloat16


def bf(x):
    return np.asarray(x, np.float32).astype(BF16)


def f64(x):
    return np.asarray(x).astype(np.float64)


E2M1 = np.array([0.0, 0.5, 1.0, 1.5, 2.0, 3.0, 4.0, 6.0, -0.0, -0.5, -1.0, -1.5, -2.0, -3.0, -4.0, -6.0])


def pack_weight(w, fmt):
    k, n = w.shape
    w = f64(bf(w)).reshape(k // 32, 32, n)
    amax = np.abs(w).max(1)
    if fmt == "e4m3":
        byte = np.frexp(amax)[1] - 1 + 127 - 7
    else:
        mant, ex = np.frexp(amax / 6.0)
        byte = np.where(mant > 0.5, ex, ex - 1) + 127
    byte = np.clip(np.where(amax > 0, byte, 1), 1, 254)
    scaled = (w * np.exp2(127.0 - byte)[:, None, :]).reshape(k, n).astype(np.float32)
    by_word = np.ascontiguousarray(scaled.reshape(k // 512, 128, 4, n).transpose(0, 1, 3, 2))
    if fmt == "e4m3":
        words = by_word.astype(ml_dtypes.float8_e4m3fn).view(np.uint8)
    else:
        c = by_word.astype(ml_dtypes.float4_e2m1fn).view(np.uint8) & 0xF
        words = c[..., 0::2] | (c[..., 1::2] << 4)
    return np.ascontiguousarray(words), np.ascontiguousarray(byte.astype(np.uint8).reshape(k // 512, 16, n))


def unpack_weight(words, scales, fmt):
    g, p, n, _ = words.shape
    if fmt == "e4m3":
        vals = np.ascontiguousarray(words).view(ml_dtypes.float8_e4m3fn).astype(np.float64)
    else:
        nib = np.empty((g, p, n, 4), np.uint8)
        nib[..., 0::2] = words & 0xF
        nib[..., 1::2] = words >> 4
        vals = E2M1[nib]
    vals = vals * np.repeat(np.exp2(scales.astype(np.float64) - 127.0), 8, axis=1)[..., None]
    return vals.transpose(0, 1, 3, 2).reshape(g * 512, n)


P, D, B = 8, 512, 128
LAMBDA = 0.1
JJ, II = np.nonzero(1 - np.eye(P, dtype=np.int64))


def setup_inputs():
    s = mx_kscale(D)
    s = s / s.max()
    F = bf(np.random.standard_normal((P, D, B)) * s[:, None])
    R = np.random.standard_normal((P, P, D, D)) / np.sqrt(D * (P - 1)) / s
    cat = np.ascontiguousarray(R.swapaxes(2, 3)).reshape(-1, D)
    words, scales = pack_weight(cat, "e4m3")
    return {"F": F, "R_words": words, "R_scales": scales}


def reference(F, R_words, R_scales):
    p = F.shape[0]
    Fq = mxq(f64(F), 1, "e4m3")
    Rq = unpack_weight(R_words, R_scales, "e4m3").reshape(P, P, D, D).swapaxes(2, 3)[II, JJ]
    Fi = Fq[II]
    agg = Rq.reshape(P, P - 1, D, D).transpose(0, 2, 1, 3).reshape(P, D, (P - 1) * D) @ Fi.reshape(P, (P - 1) * D, B)
    updated = (f64(F) + agg) / p
    M = np.zeros((P, P, D, B))
    M[II, JJ] = Rq @ Fi
    Dif = M - M.swapaxes(0, 1)
    loss = LAMBDA * 0.5 * np.sum(Dif * Dif)
    return updated, loss

@@ -1,0 +1,185 @@
+from contextlib import ExitStack
+
+import concourse.mybir as mybir
+from concourse.masks import make_identity
+
+F32 = mybir.dt.float32
+BF16 = mybir.dt.bfloat16
+I32 = mybir.dt.int32
+U32 = mybir.dt.uint32
+U8 = mybir.dt.uint8
+FP8X4 = mybir.dt.float8_e4m3fn_x4
+ALU = mybir.AluOpType
+ACT = mybir.ActivationFunctionType
+
+P = 128
+PACK = 4
+PATCHES = 8
+D = 512
+B = 128
+PAIRS = PATCHES * (PATCHES - 1) // 2
+PAIR_COLUMNS = 32
+PLANE_TILES = 4
+PLANES_PER_TILE = PATCHES * PATCHES // PLANE_TILES
+HALF = PATCHES // 2
+FINISH_AFTER = 1
+
+FLOPS = 2 * (2 * PATCHES * (PATCHES - 1) * D * D * B)
+BYTES = (
+    PATCHES * D * B * 2
+    + PATCHES * (PATCHES - 1) * (D * D + D * D // 32)
+    + PATCHES * D * B * 4
+    + 4
+)
+
+
+def tile_sheaflayer_e_kernel(tc, F, R_words, R_scales, out_0, out_1):
+    nc = tc.nc
+    with ExitStack() as ctx:
+        keep = ctx.enter_context(tc.tile_pool(name="keep", bufs=1))
+        ring = ctx.enter_context(tc.tile_pool(name="ring", bufs=4))
+        psum_sum = ctx.enter_context(tc.psum_pool(name="psum_sum", bufs=2))
+        psum_dif = ctx.enter_context(tc.psum_pool(name="psum_dif", bufs=4))
+        psum_back = ctx.enter_context(tc.psum_pool(name="psum_back", bufs=2))
+        ctx.enter_context(tc.manual_schedule())
+
+        planes = []
+        for g in range(PLANE_TILES):
+            plane_tile = keep.tile([P, PLANES_PER_TILE, D], U8, name="planes%d" % g, align_bytes=64)
+            nc.vector.memset(plane_tile[:].bitcast(I32), 0)
+            planes.append(plane_tile)
+        pair_sums = keep.tile([P, PAIR_COLUMNS], F32)
+        nc.vector.memset(pair_sums[:], 0.0)
+        ones = keep.tile([P, P], F32)
+        nc.vector.memset(ones[:], 1.0)
+        identity = keep.tile([P, P], F32)
+        make_identity(nc, identity[:])
+
+        f_rows = keep.tile([P, PATCHES, PACK, B], BF16)
+        f_dram = F.rearrange("i (p t) b -> p i (t b)", t=PACK)
+        for h in range(2):
+            four = slice(HALF * h, HALF * (h + 1))
+            nc.sync.dma_start(
+                out=f_rows[:, four].rearrange("p i t b -> p i (t b)"), in_=f_dram[:, four]
+            )
+
+        scale_dram = R_scales.rearrange("(c g) (q r) n -> g r q c n", g=PLANE_TILES, r=4)
+        words = {}
+        for j in range(PATCHES):
+            if j < PLANE_TILES:
+                for r in range(4):
+                    nc.sync.dma_start(
+                        out=planes[j][r:P:32].bitcast(I32), in_=scale_dram[j, r].bitcast(I32)
+                    )
+            for i in range(PATCHES):
+                if i == j:
+                    continue
+                block = keep.tile([P, PACK * D], U8, name="words_%d_%d" % (i, j), align_bytes=64)
+                nc.sync.dma_start(
+                    out=block[:].bitcast(I32),
+                    in_=R_words[PATCHES * i + j].rearrange("p n t -> p (n t)").bitcast(I32),
+                )
+                words[(i, j)] = block
+
+        grouped = {}
+        f_codes = {}
+        f_scales = {}
+        for sign in ("plus", "minus"):
+            grouped[sign] = keep.tile(
+                [P, PATCHES, B, PACK], BF16, name="grouped_" + sign, align_bytes=64
+            )
+            f_codes[sign] = keep.tile([P, PATCHES, B], U32, name="f_codes_" + sign, align_bytes=64)
+            f_scales[sign] = keep.tile([P, PATCHES, B], U8, name="f_scales_" + sign, align_bytes=64)
+
+        def quantise(sign, four):
+            nc.vector.quantize_mx(
+                out=f_codes[sign][:, four].rearrange("p i b -> p (i b)").bitcast(FP8X4),
+                scales=f_scales[sign][:, four].rearrange("p i b -> p (i b)"),
+                in_=grouped[sign][:, four].rearrange("p i b t -> p (i b t)"),
+            )
+
+        halves = [slice(0, HALF), slice(HALF, PATCHES)]
+        for four in halves:
+            nc.vector.tensor_copy(
+                out=grouped["plus"][:, four], in_=f_rows[:, four].rearrange("p i t b -> p i b t")
+            )
+        for four in halves:
+            quantise("plus", four)
+        for four in halves:
+            nc.vector.tensor_scalar_mul(
+                out=grouped["minus"][:, four], in0=grouped["plus"][:, four], scalar1=-1.0
+            )
+        for four in halves:
+            quantise("minus", four)
+
+        def product(bank, sign, i, j, start, stop):
+            e = PATCHES * i + j
+            nc.tensor.matmul_mx(
+                out=bank[:],
+                lhsT=f_codes[sign][:, i, :].bitcast(FP8X4),
+                lhsT_scale=f_scales[sign][:, i, :],
+                rhs=words[(i, j)][:].bitcast(FP8X4),
+                rhs_scale=planes[e % PLANE_TILES][:, e // PLANE_TILES, :],
+                start=start,
+                stop=stop,
+            )
+
+        def finish(j, sum_cols):
+            back = psum_back.tile([P, PACK, B], F32, tag="back")
+            for t in range(PACK):
+                nc.tensor.transpose(back[:, t, :], sum_cols[:, t, :], identity[:])
+            updated = keep.tile([P, PACK, B], F32, name="updated%d" % j)
+            nc.vector.scalar_tensor_tensor(
+                out=updated[:],
+                in0=f_rows[:, j],
+                scalar=1.0 / PATCHES,
+                in1=back[:],
+                op0=ALU.mult,
+                op1=ALU.add,
+            )
+            nc.sync.dma_start(
+                out=out_0[j].rearrange("(m t) b -> m (t b)", t=PACK),
+                in_=updated[:].rearrange("m t b -> m (t b)"),
+            )
+
+        pair = 0
+        waiting = None
+        for j in range(PATCHES):
+            sources = [i for i in range(PATCHES) if i != j]
+            total = psum_sum.tile([P, D], F32, tag="total")
+            for position, i in enumerate(sources):
+                product(total, "plus", i, j, start=(position == 0), stop=(position == len(sources) - 1))
+                if i < j:
+                    dif = psum_dif.tile([P, D], F32, tag="dif")
+                    product(dif, "plus", i, j, start=True, stop=False)
+                    product(dif, "minus", j, i, start=False, stop=True)
+                    squares = ring.tile([P, D], F32, tag="squares")
+                    nc.scalar.activation(
+                        out=squares[:],
+                        in_=dif[:],
+                        func=ACT.Square,
+                        accum_out=pair_sums[:, pair : pair + 1],
+                    )
+                    pair += 1
+                if position == FINISH_AFTER and waiting is not None:
+                    finish(j - 1, waiting)
+            sum_cols = ring.tile([P, PACK, P], F32, tag="sum_cols")
+            nc.vector.tensor_scalar_mul(
+                out=sum_cols[:],
+                in0=total[:].rearrange("b (m t) -> b t m", t=PACK),
+                scalar1=1.0 / PATCHES,
+            )
+            waiting = sum_cols
+        finish(PATCHES - 1, waiting)
+
+        all_rows = psum_back.tile([P, PAIR_COLUMNS], F32, tag="back")
+        nc.tensor.matmul(out=all_rows[:], lhsT=ones[:], rhs=pair_sums[:], start=True, stop=True)
+        scaled = keep.tile([P, PAIR_COLUMNS], F32)
+        loss = keep.tile([P, 1], F32)
+        nc.scalar.activation(
+            out=scaled[:], in_=all_rows[:], func=ACT.Copy, scale=0.1, accum_out=loss[:]
+        )
+        loss_cell = out_1
+        for step in range(2 - out_1.ndim):
+            loss_cell = loss_cell.unsqueeze(0)
+        nc.sync.dma_start(out=loss_cell, in_=loss[0:1, :])

@@ -64,13 +64,16 @@ def tile_sheaflayer_e_kernel(tc, F, R_words, R_scales, out_0, out_1):
             )
 
         scale_dram = R_scales.rearrange("(c g) (q r) n -> g r q c n", g=PLANE_TILES, r=4)
+        for g in range(PLANE_TILES):
+            for r in range(4):
+                live_rows = planes[g][4 * g + r : P : 32]
+                if g == 0:
+                    nc.sync.dma_start(out=live_rows.bitcast(I32), in_=scale_dram[g, r].bitcast(I32))
+                else:
+                    nc.gpsimd.dma_start(out=live_rows.bitcast(F32), in_=scale_dram[g, r].bitcast(F32))
+
         words = {}
         for j in range(PATCHES):
-            if j < PLANE_TILES:
-                for r in range(4):
-                    nc.sync.dma_start(
-                        out=planes[j][r:P:32].bitcast(I32), in_=scale_dram[j, r].bitcast(I32)
-                    )
             for i in range(PATCHES):
                 if i == j:
                     continue
@@ -100,15 +103,10 @@ def tile_sheaflayer_e_kernel(tc, F, R_words, R_scales, out_0, out_1):
 
         halves = [slice(0, HALF), slice(HALF, PATCHES)]
         for four in halves:
-            nc.vector.tensor_copy(
-                out=grouped["plus"][:, four], in_=f_rows[:, four].rearrange("p i t b -> p i b t")
-            )
-        for four in halves:
+            by_column = f_rows[:, four].rearrange("p i t b -> p i b t")
+            nc.vector.tensor_copy(out=grouped["plus"][:, four], in_=by_column)
+            nc.scalar.mul(out=grouped["minus"][:, four], in_=by_column, mul=-1.0)
             quantise("plus", four)
-        for four in halves:
-            nc.vector.tensor_scalar_mul(
-                out=grouped["minus"][:, four], in0=grouped["plus"][:, four], scalar1=-1.0
-            )
         for four in halves:
             quantise("minus", four)
 
@@ -119,7 +117,7 @@ def tile_sheaflayer_e_kernel(tc, F, R_words, R_scales, out_0, out_1):
                 lhsT=f_codes[sign][:, i, :].bitcast(FP8X4),
                 lhsT_scale=f_scales[sign][:, i, :],
                 rhs=words[(i, j)][:].bitcast(FP8X4),
-                rhs_scale=planes[e % PLANE_TILES][:, e // PLANE_TILES, :],
+                rhs_scale=planes[e % PLANE_TILES][4 * (e % PLANE_TILES) : P, e // PLANE_TILES, :],
                 start=start,
                 stop=stop,
             )

@@ -19,8 +19,7 @@ D = 512
 B = 128
 PAIRS = PATCHES * (PATCHES - 1) // 2
 PAIR_COLUMNS = 32
-PLANE_TILES = 4
-PLANES_PER_TILE = PATCHES * PATCHES // PLANE_TILES
+PLANES = 4
 HALF = PATCHES // 2
 FINISH_AFTER = 1
 
@@ -44,8 +43,8 @@ def tile_sheaflayer_e_kernel(tc, F, R_words, R_scales, out_0, out_1):
         ctx.enter_context(tc.manual_schedule())
 
         planes = []
-        for g in range(PLANE_TILES):
-            plane_tile = keep.tile([P, PLANES_PER_TILE, D], U8, name="planes%d" % g, align_bytes=64)
+        for h in range(2):
+            plane_tile = keep.tile([P, PATCHES, D], U8, name="planes%d" % h, align_bytes=64)
             nc.vector.memset(plane_tile[:].bitcast(I32), 0)
             planes.append(plane_tile)
         pair_sums = keep.tile([P, PAIR_COLUMNS], F32)
@@ -63,14 +62,19 @@ def tile_sheaflayer_e_kernel(tc, F, R_words, R_scales, out_0, out_1):
                 out=f_rows[:, four].rearrange("p i t b -> p i (t b)"), in_=f_dram[:, four]
             )
 
-        scale_dram = R_scales.rearrange("(c g) (q r) n -> g r q c n", g=PLANE_TILES, r=4)
-        for g in range(PLANE_TILES):
-            for r in range(4):
-                live_rows = planes[g][4 * g + r : P : 32]
-                if g == 0:
-                    nc.sync.dma_start(out=live_rows.bitcast(I32), in_=scale_dram[g, r].bitcast(I32))
-                else:
-                    nc.gpsimd.dma_start(out=live_rows.bitcast(F32), in_=scale_dram[g, r].bitcast(F32))
+        scale_dram = R_scales.rearrange("(i h o) (q r) n -> h q r o i n", h=2, o=PLANES, r=4)
+        for h in range(2):
+            for q in range(4):
+                for r in range(4):
+                    live_rows = planes[h][32 * q + r : 32 * q + 4 * PLANES : 4]
+                    if h == 0:
+                        nc.sync.dma_start(
+                            out=live_rows.bitcast(I32), in_=scale_dram[h, q, r].bitcast(I32)
+                        )
+                    else:
+                        nc.gpsimd.dma_start(
+                            out=live_rows.bitcast(F32), in_=scale_dram[h, q, r].bitcast(F32)
+                        )
 
         words = {}
         for j in range(PATCHES):
@@ -111,13 +115,12 @@ def tile_sheaflayer_e_kernel(tc, F, R_words, R_scales, out_0, out_1):
             quantise("minus", four)
 
         def product(bank, sign, i, j, start, stop):
-            e = PATCHES * i + j
             nc.tensor.matmul_mx(
                 out=bank[:],
                 lhsT=f_codes[sign][:, i, :].bitcast(FP8X4),
                 lhsT_scale=f_scales[sign][:, i, :],
                 rhs=words[(i, j)][:].bitcast(FP8X4),
-                rhs_scale=planes[e % PLANE_TILES][4 * (e % PLANE_TILES) : P, e // PLANE_TILES, :],
+                rhs_scale=planes[j // PLANES][4 * (j % PLANES) : P, i, :],
                 start=start,
                 stop=stop,
             )

@@ -21,6 +21,7 @@ PAIRS = PATCHES * (PATCHES - 1) // 2
 PAIR_COLUMNS = 32
 PLANES = 4
 HALF = PATCHES // 2
+SECOND_PLANES_AFTER = 6
 FINISH_AFTER = 1
 
 FLOPS = 2 * (2 * PATCHES * (PATCHES - 1) * D * D * B)
@@ -63,18 +64,14 @@ def tile_sheaflayer_e_kernel(tc, F, R_words, R_scales, out_0, out_1):
             )
 
         scale_dram = R_scales.rearrange("(i h o) (q r) n -> h q r o i n", h=2, o=PLANES, r=4)
-        for h in range(2):
-            for q in range(4):
-                for r in range(4):
-                    live_rows = planes[h][32 * q + r : 32 * q + 4 * PLANES : 4]
-                    if h == 0:
-                        nc.sync.dma_start(
-                            out=live_rows.bitcast(I32), in_=scale_dram[h, q, r].bitcast(I32)
-                        )
-                    else:
-                        nc.gpsimd.dma_start(
-                            out=live_rows.bitcast(F32), in_=scale_dram[h, q, r].bitcast(F32)
-                        )
+
+        def load_scales(h, row):
+            q, r = row // 4, row % 4
+            live_rows = planes[h][32 * q + r : 32 * q + 4 * PLANES : 4]
+            nc.sync.dma_start(out=live_rows.bitcast(I32), in_=scale_dram[h, q, r].bitcast(I32))
+
+        for row in range(16):
+            load_scales(0, row)
 
         words = {}
         for j in range(PATCHES):
@@ -87,6 +84,9 @@ def tile_sheaflayer_e_kernel(tc, F, R_words, R_scales, out_0, out_1):
                     in_=R_words[PATCHES * i + j].rearrange("p n t -> p (n t)").bitcast(I32),
                 )
                 words[(i, j)] = block
+                row = len(words) - 1 - SECOND_PLANES_AFTER
+                if row >= 0 and row < 16:
+                    load_scales(1, row)
 
         grouped = {}
         f_codes = {}

@@ -17,12 +17,15 @@ PACK = 4
 PATCHES = 8
 D = 512
 B = 128
-PAIRS = PATCHES * (PATCHES - 1) // 2
-PAIR_COLUMNS = 32
 PLANES = 4
 HALF = PATCHES // 2
-SECOND_PLANES_AFTER = 6
-FINISH_AFTER = 1
+LOW = list(range(HALF))
+HIGH = list(range(HALF, PATCHES))
+INSIDE_LOW = [(i, j) for i in LOW for j in LOW if i < j]
+ACROSS = [(i, j) for j in HIGH for i in LOW]
+INSIDE_HIGH = [(i, j) for i in HIGH for j in HIGH if i < j]
+PAIRS = INSIDE_LOW + ACROSS + INSIDE_HIGH
+PAIR_COLUMNS = 32
 
 FLOPS = 2 * (2 * PATCHES * (PATCHES - 1) * D * D * B)
 BYTES = (
@@ -38,9 +41,7 @@ def tile_sheaflayer_e_kernel(tc, F, R_words, R_scales, out_0, out_1):
     with ExitStack() as ctx:
         keep = ctx.enter_context(tc.tile_pool(name="keep", bufs=1))
         ring = ctx.enter_context(tc.tile_pool(name="ring", bufs=4))
-        psum_sum = ctx.enter_context(tc.psum_pool(name="psum_sum", bufs=2))
-        psum_dif = ctx.enter_context(tc.psum_pool(name="psum_dif", bufs=4))
-        psum_back = ctx.enter_context(tc.psum_pool(name="psum_back", bufs=2))
+        psum = ctx.enter_context(tc.psum_pool(name="psum", bufs=1))
         ctx.enter_context(tc.manual_schedule())
 
         planes = []
@@ -52,41 +53,46 @@ def tile_sheaflayer_e_kernel(tc, F, R_words, R_scales, out_0, out_1):
         nc.vector.memset(pair_sums[:], 0.0)
         ones = keep.tile([P, P], F32)
         nc.vector.memset(ones[:], 1.0)
-        identity = keep.tile([P, P], F32)
-        make_identity(nc, identity[:])
 
         f_rows = keep.tile([P, PATCHES, PACK, B], BF16)
         f_dram = F.rearrange("i (p t) b -> p i (t b)", t=PACK)
+        halves = [slice(0, HALF), slice(HALF, PATCHES)]
         for h in range(2):
-            four = slice(HALF * h, HALF * (h + 1))
             nc.sync.dma_start(
-                out=f_rows[:, four].rearrange("p i t b -> p i (t b)"), in_=f_dram[:, four]
+                out=f_rows[:, halves[h]].rearrange("p i t b -> p i (t b)"), in_=f_dram[:, halves[h]]
+            )
+        identity = keep.tile([P, P], F32)
+        make_identity(nc, identity[:])
+
+        scale_dram = R_scales.rearrange("(h o j) (q r) n -> h q r o j n", h=2, o=PLANES, r=4)
+
+        def load_scales(h, js, row):
+            q, r = row // 4, row % 4
+            nc.sync.dma_start(
+                out=planes[h][32 * q + r : 32 * q + 4 * PLANES : 4, js].bitcast(I32),
+                in_=scale_dram[h, q, r][:, js].bitcast(I32),
             )
 
-        scale_dram = R_scales.rearrange("(i h o) (q r) n -> h q r o i n", h=2, o=PLANES, r=4)
-
-        def load_scales(h, row):
-            q, r = row // 4, row % 4
-            live_rows = planes[h][32 * q + r : 32 * q + 4 * PLANES : 4]
-            nc.sync.dma_start(out=live_rows.bitcast(I32), in_=scale_dram[h, q, r].bitcast(I32))
-
         for row in range(16):
-            load_scales(0, row)
+            load_scales(0, slice(0, PATCHES), row)
 
         words = {}
-        for j in range(PATCHES):
-            for i in range(PATCHES):
-                if i == j:
-                    continue
-                block = keep.tile([P, PACK * D], U8, name="words_%d_%d" % (i, j), align_bytes=64)
-                nc.sync.dma_start(
-                    out=block[:].bitcast(I32),
-                    in_=R_words[PATCHES * i + j].rearrange("p n t -> p (n t)").bitcast(I32),
-                )
-                words[(i, j)] = block
-                row = len(words) - 1 - SECOND_PLANES_AFTER
-                if row >= 0 and row < 16:
-                    load_scales(1, row)
+        blocks = []
+        for i, j in PAIRS:
+            blocks += [(i, j), (j, i)]
+        later_rows = {}
+        for row in range(16):
+            later_rows.setdefault(1 + row // 2, []).append((halves[0], row))
+            later_rows.setdefault(12 + row, []).append((halves[1], row))
+        for position, (i, j) in enumerate(blocks):
+            block = keep.tile([P, PACK * D], U8, name="words_%d_%d" % (i, j), align_bytes=64)
+            nc.sync.dma_start(
+                out=block[:].bitcast(I32),
+                in_=R_words[PATCHES * i + j].rearrange("p n t -> p (n t)").bitcast(I32),
+            )
+            words[(i, j)] = block
+            for js, row in later_rows.get(position, []):
+                load_scales(1, js, row)
 
         grouped = {}
         f_codes = {}
@@ -98,6 +104,13 @@ def tile_sheaflayer_e_kernel(tc, F, R_words, R_scales, out_0, out_1):
             f_codes[sign] = keep.tile([P, PATCHES, B], U32, name="f_codes_" + sign, align_bytes=64)
             f_scales[sign] = keep.tile([P, PATCHES, B], U8, name="f_scales_" + sign, align_bytes=64)
 
+        def regroup(sign, four):
+            by_column = f_rows[:, four].rearrange("p i t b -> p i b t")
+            if sign == "plus":
+                nc.vector.tensor_copy(out=grouped[sign][:, four], in_=by_column)
+            else:
+                nc.scalar.mul(out=grouped[sign][:, four], in_=by_column, mul=-1.0)
+
         def quantise(sign, four):
             nc.vector.quantize_mx(
                 out=f_codes[sign][:, four].rearrange("p i b -> p (i b)").bitcast(FP8X4),
@@ -105,14 +118,17 @@ def tile_sheaflayer_e_kernel(tc, F, R_words, R_scales, out_0, out_1):
                 in_=grouped[sign][:, four].rearrange("p i b t -> p (i b t)"),
             )
 
-        halves = [slice(0, HALF), slice(HALF, PATCHES)]
         for four in halves:
-            by_column = f_rows[:, four].rearrange("p i t b -> p i b t")
-            nc.vector.tensor_copy(out=grouped["plus"][:, four], in_=by_column)
-            nc.scalar.mul(out=grouped["minus"][:, four], in_=by_column, mul=-1.0)
+            regroup("plus", four)
+            regroup("minus", four)
             quantise("plus", four)
         for four in halves:
             quantise("minus", four)
+
+        group = {}
+
+        def bank_tile(bank, name):
+            return psum.tile([P, D], F32, tag="bank%d" % bank, name=name)
 
         def product(bank, sign, i, j, start, stop):
             nc.tensor.matmul_mx(
@@ -120,21 +136,78 @@ def tile_sheaflayer_e_kernel(tc, F, R_words, R_scales, out_0, out_1):
                 lhsT=f_codes[sign][:, i, :].bitcast(FP8X4),
                 lhsT_scale=f_scales[sign][:, i, :],
                 rhs=words[(i, j)][:].bitcast(FP8X4),
-                rhs_scale=planes[j // PLANES][4 * (j % PLANES) : P, i, :],
+                rhs_scale=planes[i // PLANES][4 * (i % PLANES) : P, j, :],
                 start=start,
                 stop=stop,
             )
 
-        def finish(j, sum_cols):
-            back = psum_back.tile([P, PACK, B], F32, tag="back")
+        def open_sum(j, bank, passes):
+            group[j] = [bank_tile(bank, "sum%d_in_%d" % (j, bank)), 0, passes]
+
+        def add_to_sum(i, j):
+            bank, done, passes = group[j]
+            product(bank, "plus", i, j, start=(done == 0), stop=(done == passes - 1))
+            group[j][1] = done + 1
+
+        def pair_passes(index, dif_bank):
+            i, j = PAIRS[index]
+            dif = bank_tile(dif_bank, "dif%d" % index)
+            add_to_sum(i, j)
+            product(dif, "plus", i, j, start=True, stop=False)
+            add_to_sum(j, i)
+            product(dif, "minus", j, i, start=False, stop=True)
+            squares = ring.tile([P, D], F32, tag="squares", name="squares%d" % index)
+            nc.scalar.activation(
+                out=squares[:],
+                in_=dif[:],
+                func=ACT.Square,
+                accum_out=pair_sums[:, index : index + 1],
+            )
+
+        parked = {}
+        sum_cols = {}
+
+        def empty(j):
+            bank = group[j][0]
+            by_t = bank[:].rearrange("b (m t) -> b t m", t=PACK)
+            cols = ring.tile([P, PACK, P], F32, tag="sum_cols", name="sum_cols%d" % j)
+            if j in parked:
+                nc.vector.scalar_tensor_tensor(
+                    out=cols[:],
+                    in0=by_t,
+                    scalar=1.0 / PATCHES,
+                    in1=parked[j][:],
+                    op0=ALU.mult,
+                    op1=ALU.add,
+                )
+            else:
+                nc.vector.tensor_scalar_mul(out=cols[:], in0=by_t, scalar1=1.0 / PATCHES)
+            sum_cols[j] = cols
+
+        def park(j):
+            cols = keep.tile([P, PACK, P], F32, name="parked%d" % j)
+            nc.vector.tensor_scalar_mul(
+                out=cols[:],
+                in0=group[j][0][:].rearrange("b (m t) -> b t m", t=PACK),
+                scalar1=1.0 / PATCHES,
+            )
+            parked[j] = cols
+
+        backs = {}
+
+        def turn_back(j, bank):
+            back = psum.tile([P, PACK, B], F32, tag="bank%d" % bank, name="back%d" % j)
             for t in range(PACK):
-                nc.tensor.transpose(back[:, t, :], sum_cols[:, t, :], identity[:])
+                nc.tensor.transpose(back[:, t, :], sum_cols[j][:, t, :], identity[:])
+            backs[j] = back
+
+        def finish(j):
             updated = keep.tile([P, PACK, B], F32, name="updated%d" % j)
             nc.vector.scalar_tensor_tensor(
                 out=updated[:],
                 in0=f_rows[:, j],
                 scalar=1.0 / PATCHES,
-                in1=back[:],
+                in1=backs[j][:],
                 op0=ALU.mult,
                 op1=ALU.add,
             )
@@ -143,37 +216,45 @@ def tile_sheaflayer_e_kernel(tc, F, R_words, R_scales, out_0, out_1):
                 in_=updated[:].rearrange("m t b -> m (t b)"),
             )
 
-        pair = 0
-        waiting = None
-        for j in range(PATCHES):
-            sources = [i for i in range(PATCHES) if i != j]
-            total = psum_sum.tile([P, D], F32, tag="total")
-            for position, i in enumerate(sources):
-                product(total, "plus", i, j, start=(position == 0), stop=(position == len(sources) - 1))
-                if i < j:
-                    dif = psum_dif.tile([P, D], F32, tag="dif")
-                    product(dif, "plus", i, j, start=True, stop=False)
-                    product(dif, "minus", j, i, start=False, stop=True)
-                    squares = ring.tile([P, D], F32, tag="squares")
-                    nc.scalar.activation(
-                        out=squares[:],
-                        in_=dif[:],
-                        func=ACT.Square,
-                        accum_out=pair_sums[:, pair : pair + 1],
-                    )
-                    pair += 1
-                if position == FINISH_AFTER and waiting is not None:
-                    finish(j - 1, waiting)
-            sum_cols = ring.tile([P, PACK, P], F32, tag="sum_cols")
-            nc.vector.tensor_scalar_mul(
-                out=sum_cols[:],
-                in0=total[:].rearrange("b (m t) -> b t m", t=PACK),
-                scalar1=1.0 / PATCHES,
-            )
-            waiting = sum_cols
-        finish(PATCHES - 1, waiting)
+        for j in LOW:
+            open_sum(j, j, PATCHES - 1)
+        for index in range(len(INSIDE_LOW)):
+            pair_passes(index, 4 + index % 4)
+        index = len(INSIDE_LOW)
+        for j in HIGH:
+            open_sum(j, 6 + j % 2, HALF if j < 6 else PATCHES - 1)
+            for i in LOW:
+                pair_passes(index, 4 + index % 2)
+                index += 1
+                if j == PATCHES - 1:
+                    empty(i)
+            if j < 6:
+                park(j)
+        for j in (4, 5):
+            open_sum(j, j - 4, PATCHES - 1 - HALF)
+        for step, (i, j) in enumerate(INSIDE_HIGH):
+            pair_passes(index, 4 + index % 2)
+            index += 1
+            if step == 1 or step == 2:
+                for c in (2 * step - 2, 2 * step - 1):
+                    turn_back(c, 2 + c % 2)
+                for c in (2 * step - 2, 2 * step - 1):
+                    finish(c)
+            if step == 2:
+                empty(4)
+            if step == 3:
+                turn_back(4, 2)
+                finish(4)
+            if step == 4:
+                empty(5)
+        empty(6)
+        empty(7)
+        for c in (5, 6, 7):
+            turn_back(c, {5: 3, 6: 2, 7: 0}[c])
+        for c in (5, 6, 7):
+            finish(c)
 
-        all_rows = psum_back.tile([P, PAIR_COLUMNS], F32, tag="back")
+        all_rows = psum.tile([P, PAIR_COLUMNS], F32, tag="bank4", name="all_rows")
         nc.tensor.matmul(out=all_rows[:], lhsT=ones[:], rhs=pair_sums[:], start=True, stop=True)
         scaled = keep.tile([P, PAIR_COLUMNS], F32)
         loss = keep.tile([P, 1], F32)

@@ -44,11 +44,12 @@ def tile_sheaflayer_e_kernel(tc, F, R_words, R_scales, out_0, out_1):
         psum = ctx.enter_context(tc.psum_pool(name="psum", bufs=1))
         ctx.enter_context(tc.manual_schedule())
 
-        planes = []
+        planes = {}
         for h in range(2):
-            plane_tile = keep.tile([P, PATCHES, D], U8, name="planes%d" % h, align_bytes=64)
-            nc.vector.memset(plane_tile[:].bitcast(I32), 0)
-            planes.append(plane_tile)
+            for g in range(2):
+                plane_tile = keep.tile([P, HALF, D], U8, name="planes%d%d" % (h, g), align_bytes=64)
+                nc.vector.memset(plane_tile[:].bitcast(I32), 0)
+                planes[(h, g)] = plane_tile
         pair_sums = keep.tile([P, PAIR_COLUMNS], F32)
         nc.vector.memset(pair_sums[:], 0.0)
         ones = keep.tile([P, P], F32)
@@ -66,15 +67,15 @@ def tile_sheaflayer_e_kernel(tc, F, R_words, R_scales, out_0, out_1):
 
         scale_dram = R_scales.rearrange("(h o j) (q r) n -> h q r o j n", h=2, o=PLANES, r=4)
 
-        def load_scales(h, js, row):
+        def load_scales(h, g, row):
             q, r = row // 4, row % 4
             nc.sync.dma_start(
-                out=planes[h][32 * q + r : 32 * q + 4 * PLANES : 4, js].bitcast(I32),
-                in_=scale_dram[h, q, r][:, js].bitcast(I32),
+                out=planes[(h, g)][32 * q + r : 32 * q + 4 * PLANES : 4].bitcast(I32),
+                in_=scale_dram[h, q, r][:, HALF * g : HALF * (g + 1)].bitcast(I32),
             )
 
         for row in range(16):
-            load_scales(0, slice(0, PATCHES), row)
+            load_scales(0, 0, row)
 
         words = {}
         blocks = []
@@ -82,8 +83,9 @@ def tile_sheaflayer_e_kernel(tc, F, R_words, R_scales, out_0, out_1):
             blocks += [(i, j), (j, i)]
         later_rows = {}
         for row in range(16):
-            later_rows.setdefault(1 + row // 2, []).append((halves[0], row))
-            later_rows.setdefault(12 + row, []).append((halves[1], row))
+            later_rows.setdefault(1 + row // 2, []).append((0, 1, row))
+            later_rows.setdefault(1 + row // 2, []).append((1, 0, row))
+            later_rows.setdefault(12 + row, []).append((1, 1, row))
         for position, (i, j) in enumerate(blocks):
             block = keep.tile([P, PACK * D], U8, name="words_%d_%d" % (i, j), align_bytes=64)
             nc.sync.dma_start(
@@ -91,8 +93,8 @@ def tile_sheaflayer_e_kernel(tc, F, R_words, R_scales, out_0, out_1):
                 in_=R_words[PATCHES * i + j].rearrange("p n t -> p (n t)").bitcast(I32),
             )
             words[(i, j)] = block
-            for js, row in later_rows.get(position, []):
-                load_scales(1, js, row)
+            for h, g, row in later_rows.get(position, []):
+                load_scales(h, g, row)
 
         grouped = {}
         f_codes = {}
@@ -136,7 +138,7 @@ def tile_sheaflayer_e_kernel(tc, F, R_words, R_scales, out_0, out_1):
                 lhsT=f_codes[sign][:, i, :].bitcast(FP8X4),
                 lhsT_scale=f_scales[sign][:, i, :],
                 rhs=words[(i, j)][:].bitcast(FP8X4),
-                rhs_scale=planes[i // PLANES][4 * (i % PLANES) : P, j, :],
+                rhs_scale=planes[(i // HALF, j // HALF)][4 * (i % HALF) : P, j % HALF, :],
                 start=start,
                 stop=stop,
             )

@@ -19,12 +19,19 @@ D = 512
 B = 128
 PLANES = 4
 HALF = PATCHES // 2
+BY_GPSIMD = (0, 1, 2, 3, 4)
+BY_SYNC = (5, 6, 7)
 LOW = list(range(HALF))
 HIGH = list(range(HALF, PATCHES))
 INSIDE_LOW = [(i, j) for i in LOW for j in LOW if i < j]
-ACROSS = [(i, j) for j in HIGH for i in LOW]
+ACROSS = [(i, j) for i in LOW for j in HIGH]
 INSIDE_HIGH = [(i, j) for i in HIGH for j in HIGH if i < j]
 PAIRS = INSIDE_LOW + ACROSS + INSIDE_HIGH
+SYNC_SCALES_AFTER = 24
+PREPARE_AT = 1
+TURN_AT = 5
+LATE_F = 2
+BY_SCALAR = 7
 PAIR_COLUMNS = 32
 
 FLOPS = 2 * (2 * PATCHES * (PATCHES - 1) * D * D * B)
@@ -44,12 +51,13 @@ def tile_sheaflayer_e_kernel(tc, F, R_words, R_scales, out_0, out_1):
         psum = ctx.enter_context(tc.psum_pool(name="psum", bufs=1))
         ctx.enter_context(tc.manual_schedule())
 
-        planes = {}
-        for h in range(2):
-            for g in range(2):
-                plane_tile = keep.tile([P, HALF, D], U8, name="planes%d%d" % (h, g), align_bytes=64)
-                nc.vector.memset(plane_tile[:].bitcast(I32), 0)
-                planes[(h, g)] = plane_tile
+        low_planes = keep.tile([P, PATCHES, D], U8, align_bytes=64)
+        nc.vector.memset(low_planes[:].bitcast(I32), 0)
+        high_planes = []
+        for j in range(PATCHES):
+            plane_tile = keep.tile([P, D], U8, name="high_planes%d" % j, align_bytes=64)
+            nc.vector.memset(plane_tile[:].bitcast(I32), 0)
+            high_planes.append(plane_tile)
         pair_sums = keep.tile([P, PAIR_COLUMNS], F32)
         nc.vector.memset(pair_sums[:], 0.0)
         ones = keep.tile([P, P], F32)
@@ -58,43 +66,56 @@ def tile_sheaflayer_e_kernel(tc, F, R_words, R_scales, out_0, out_1):
         f_rows = keep.tile([P, PATCHES, PACK, B], BF16)
         f_dram = F.rearrange("i (p t) b -> p i (t b)", t=PACK)
         halves = [slice(0, HALF), slice(HALF, PATCHES)]
-        for h in range(2):
+
+        def load_f(half):
             nc.sync.dma_start(
-                out=f_rows[:, halves[h]].rearrange("p i t b -> p i (t b)"), in_=f_dram[:, halves[h]]
+                out=f_rows[:, half].rearrange("p i t b -> p i (t b)"), in_=f_dram[:, half]
             )
+
         identity = keep.tile([P, P], F32)
         make_identity(nc, identity[:])
 
-        scale_dram = R_scales.rearrange("(h o j) (q r) n -> h q r o j n", h=2, o=PLANES, r=4)
+        low_dram = R_scales.rearrange("(h o j) (q r) n -> h q r o j n", h=2, o=PLANES, r=4)
+        high_dram = R_scales.rearrange("(h o j) (q r) n -> h j q o r n", h=2, o=PLANES, r=4)
 
-        def load_scales(h, g, row):
+        def load_low_scales(row):
             q, r = row // 4, row % 4
             nc.sync.dma_start(
-                out=planes[(h, g)][32 * q + r : 32 * q + 4 * PLANES : 4].bitcast(I32),
-                in_=scale_dram[h, q, r][:, HALF * g : HALF * (g + 1)].bitcast(I32),
+                out=low_planes[32 * q + r : 32 * q + 4 * PLANES : 4].bitcast(I32),
+                in_=low_dram[0, q, r].bitcast(I32),
             )
 
+        def load_high_scales(queue, dtype, j, q):
+            queue.dma_start(
+                out=high_planes[j][32 * q : 32 * q + 4 * PLANES].bitcast(dtype),
+                in_=high_dram[1, j, q].bitcast(dtype),
+            )
+
+        load_f(halves[0])
         for row in range(16):
-            load_scales(0, 0, row)
+            load_low_scales(row)
+        for j in BY_GPSIMD:
+            for q in range(4):
+                load_high_scales(nc.gpsimd, F32, j, q)
 
         words = {}
         blocks = []
         for i, j in PAIRS:
             blocks += [(i, j), (j, i)]
-        later_rows = {}
-        for row in range(16):
-            later_rows.setdefault(1 + row // 2, []).append((0, 1, row))
-            later_rows.setdefault(1 + row // 2, []).append((1, 0, row))
-            later_rows.setdefault(12 + row, []).append((1, 1, row))
+        scales_behind = {}
+        for number, (j, q) in enumerate([(j, q) for j in BY_SYNC for q in range(4)]):
+            scales_behind[SYNC_SCALES_AFTER + number] = (j, q)
         for position, (i, j) in enumerate(blocks):
+            if position == LATE_F:
+                load_f(halves[1])
             block = keep.tile([P, PACK * D], U8, name="words_%d_%d" % (i, j), align_bytes=64)
             nc.sync.dma_start(
                 out=block[:].bitcast(I32),
                 in_=R_words[PATCHES * i + j].rearrange("p n t -> p (n t)").bitcast(I32),
             )
             words[(i, j)] = block
-            for h, g, row in later_rows.get(position, []):
-                load_scales(h, g, row)
+            if position in scales_behind:
+                load_high_scales(nc.sync, I32, *scales_behind[position])
 
         grouped = {}
         f_codes = {}
@@ -120,17 +141,23 @@ def tile_sheaflayer_e_kernel(tc, F, R_words, R_scales, out_0, out_1):
                 in_=grouped[sign][:, four].rearrange("p i b t -> p (i b t)"),
             )
 
-        for four in halves:
+        def prepare(four):
             regroup("plus", four)
             regroup("minus", four)
             quantise("plus", four)
-        for four in halves:
             quantise("minus", four)
+
+        prepare(halves[0])
 
         group = {}
 
         def bank_tile(bank, name):
             return psum.tile([P, D], F32, tag="bank%d" % bank, name=name)
+
+        def plane(i, j):
+            if i < HALF:
+                return low_planes[4 * i : P, j, :]
+            return high_planes[j][4 * (i % HALF) : P, :]
 
         def product(bank, sign, i, j, start, stop):
             nc.tensor.matmul_mx(
@@ -138,26 +165,21 @@ def tile_sheaflayer_e_kernel(tc, F, R_words, R_scales, out_0, out_1):
                 lhsT=f_codes[sign][:, i, :].bitcast(FP8X4),
                 lhsT_scale=f_scales[sign][:, i, :],
                 rhs=words[(i, j)][:].bitcast(FP8X4),
-                rhs_scale=planes[(i // HALF, j // HALF)][4 * (i % HALF) : P, j % HALF, :],
+                rhs_scale=plane(i, j),
                 start=start,
                 stop=stop,
             )
 
         def open_sum(j, bank, passes):
-            group[j] = [bank_tile(bank, "sum%d_in_%d" % (j, bank)), 0, passes]
+            group[j] = [bank_tile(bank, "sum%d_of_%d" % (j, passes)), 0, passes]
 
         def add_to_sum(i, j):
             bank, done, passes = group[j]
             product(bank, "plus", i, j, start=(done == 0), stop=(done == passes - 1))
             group[j][1] = done + 1
 
-        def pair_passes(index, dif_bank):
-            i, j = PAIRS[index]
-            dif = bank_tile(dif_bank, "dif%d" % index)
-            add_to_sum(i, j)
-            product(dif, "plus", i, j, start=True, stop=False)
-            add_to_sum(j, i)
-            product(dif, "minus", j, i, start=False, stop=True)
+        def square(pair, dif):
+            index = PAIRS.index(pair)
             squares = ring.tile([P, D], F32, tag="squares", name="squares%d" % index)
             nc.scalar.activation(
                 out=squares[:],
@@ -166,12 +188,22 @@ def tile_sheaflayer_e_kernel(tc, F, R_words, R_scales, out_0, out_1):
                 accum_out=pair_sums[:, index : index + 1],
             )
 
+        def pair_passes(i, j, dif_bank):
+            dif = bank_tile(dif_bank, "dif%d%d" % (i, j))
+            add_to_sum(i, j)
+            product(dif, "plus", i, j, start=True, stop=False)
+            add_to_sum(j, i)
+            if (i, j) == PAIRS[-1]:
+                empty(j)
+                empty(i)
+            product(dif, "minus", j, i, start=False, stop=True)
+            square((i, j), dif)
+
         parked = {}
         sum_cols = {}
 
         def empty(j):
-            bank = group[j][0]
-            by_t = bank[:].rearrange("b (m t) -> b t m", t=PACK)
+            by_t = group[j][0][:].rearrange("b (m t) -> b t m", t=PACK)
             cols = ring.tile([P, PACK, P], F32, tag="sum_cols", name="sum_cols%d" % j)
             if j in parked:
                 nc.vector.scalar_tensor_tensor(
@@ -182,18 +214,26 @@ def tile_sheaflayer_e_kernel(tc, F, R_words, R_scales, out_0, out_1):
                     op0=ALU.mult,
                     op1=ALU.add,
                 )
+            elif j == BY_SCALAR:
+                nc.scalar.mul(out=cols[:], in_=by_t, mul=1.0 / PATCHES)
             else:
                 nc.vector.tensor_scalar_mul(out=cols[:], in0=by_t, scalar1=1.0 / PATCHES)
             sum_cols[j] = cols
 
-        def park(j):
-            cols = keep.tile([P, PACK, P], F32, name="parked%d" % j)
-            nc.vector.tensor_scalar_mul(
-                out=cols[:],
-                in0=group[j][0][:].rearrange("b (m t) -> b t m", t=PACK),
-                scalar1=1.0 / PATCHES,
-            )
-            parked[j] = cols
+        def park(j, block):
+            by_t = block[:].rearrange("b (m t) -> b t m", t=PACK)
+            if j not in parked:
+                parked[j] = keep.tile([P, PACK, P], F32, name="parked%d" % j)
+                nc.vector.tensor_scalar_mul(out=parked[j][:], in0=by_t, scalar1=1.0 / PATCHES)
+            else:
+                nc.vector.scalar_tensor_tensor(
+                    out=parked[j][:],
+                    in0=by_t,
+                    scalar=1.0 / PATCHES,
+                    in1=parked[j][:],
+                    op0=ALU.mult,
+                    op1=ALU.add,
+                )
 
         backs = {}
 
@@ -219,44 +259,43 @@ def tile_sheaflayer_e_kernel(tc, F, R_words, R_scales, out_0, out_1):
             )
 
         for j in LOW:
-            open_sum(j, j, PATCHES - 1)
-        for index in range(len(INSIDE_LOW)):
-            pair_passes(index, 4 + index % 4)
-        index = len(INSIDE_LOW)
+            open_sum(j, j, HALF - 1)
+        for step, (i, j) in enumerate(INSIDE_LOW):
+            pair_passes(i, j, 4 + step % 4)
+            if step == PREPARE_AT:
+                prepare(halves[1])
+            if j == HALF - 1:
+                park(i, group[i][0])
+        park(HALF - 1, group[HALF - 1][0])
         for j in HIGH:
-            open_sum(j, 6 + j % 2, HALF if j < 6 else PATCHES - 1)
-            for i in LOW:
-                pair_passes(index, 4 + index % 2)
-                index += 1
-                if j == PATCHES - 1:
-                    empty(i)
-            if j < 6:
-                park(j)
-        for j in (4, 5):
-            open_sum(j, j - 4, PATCHES - 1 - HALF)
+            open_sum(j, 4 + (j + 2) % HALF, PATCHES - 1)
+        count = 0
+        for i in LOW:
+            open_sum(i, 3 * (i % 2), HALF)
+            for j in HIGH:
+                pair_passes(i, j, 1 + count % 2)
+                count += 1
+                if j == TURN_AT and i > 0:
+                    turn_back(i - 1, 3 * ((i - 1) % 2))
+                    finish(i - 1)
+            empty(i)
         for step, (i, j) in enumerate(INSIDE_HIGH):
-            pair_passes(index, 4 + index % 2)
-            index += 1
-            if step == 1 or step == 2:
-                for c in (2 * step - 2, 2 * step - 1):
-                    turn_back(c, 2 + c % 2)
-                for c in (2 * step - 2, 2 * step - 1):
-                    finish(c)
-            if step == 2:
-                empty(4)
+            pair_passes(i, j, 1 + count % 2)
+            count += 1
+            if step == 0:
+                turn_back(3, 3)
+                finish(3)
+            if j == PATCHES - 1 and i < 6:
+                empty(i)
             if step == 3:
-                turn_back(4, 2)
+                turn_back(4, 0)
                 finish(4)
-            if step == 4:
-                empty(5)
-        empty(6)
-        empty(7)
-        for c in (5, 6, 7):
-            turn_back(c, {5: 3, 6: 2, 7: 0}[c])
-        for c in (5, 6, 7):
+        for c, bank in ((5, 3), (7, 0), (6, 6)):
+            turn_back(c, bank)
+        for c in (5, 7, 6):
             finish(c)
 
-        all_rows = psum.tile([P, PAIR_COLUMNS], F32, tag="bank4", name="all_rows")
+        all_rows = psum.tile([P, PAIR_COLUMNS], F32, tag="bank1", name="all_rows")
         nc.tensor.matmul(out=all_rows[:], lhsT=ones[:], rhs=pair_sums[:], start=True, stop=True)
         scaled = keep.tile([P, PAIR_COLUMNS], F32)
         loss = keep.tile([P, 1], F32)

@@ -24,14 +24,18 @@ BY_SYNC = (5, 6, 7)
 LOW = list(range(HALF))
 HIGH = list(range(HALF, PATCHES))
 INSIDE_LOW = [(i, j) for i in LOW for j in LOW if i < j]
-ACROSS = [(i, j) for i in LOW for j in HIGH]
+ORDER = (4, 5, 7, 6)
+LIGHT = [(i, 7) for i in LOW]
+ACROSS = [(i, j) for i in LOW for j in ORDER]
 INSIDE_HIGH = [(i, j) for i in HIGH for j in HIGH if i < j]
 PAIRS = INSIDE_LOW + ACROSS + INSIDE_HIGH
+LAST_ROWS = 4
+LAST_BEHIND = 0
 SYNC_SCALES_AFTER = 24
-PREPARE_AT = 1
+PREPARE_AT = 0
 TURN_AT = 5
 LATE_F = 2
-BY_SCALAR = 7
+BY_SCALAR = 6
 PAIR_COLUMNS = 32
 
 FLOPS = 2 * (2 * PATCHES * (PATCHES - 1) * D * D * B)
@@ -92,7 +96,7 @@ def tile_sheaflayer_e_kernel(tc, F, R_words, R_scales, out_0, out_1):
             )
 
         load_f(halves[0])
-        for row in range(16):
+        for row in range(16 - LAST_ROWS):
             load_low_scales(row)
         for j in BY_GPSIMD:
             for q in range(4):
@@ -114,6 +118,9 @@ def tile_sheaflayer_e_kernel(tc, F, R_words, R_scales, out_0, out_1):
                 in_=R_words[PATCHES * i + j].rearrange("p n t -> p (n t)").bitcast(I32),
             )
             words[(i, j)] = block
+            if position == LAST_BEHIND:
+                for row in range(16 - LAST_ROWS, 16):
+                    load_low_scales(row)
             if position in scales_behind:
                 load_high_scales(nc.sync, I32, *scales_behind[position])
 
@@ -193,11 +200,22 @@ def tile_sheaflayer_e_kernel(tc, F, R_words, R_scales, out_0, out_1):
             add_to_sum(i, j)
             product(dif, "plus", i, j, start=True, stop=False)
             add_to_sum(j, i)
-            if (i, j) == PAIRS[-1]:
-                empty(j)
-                empty(i)
             product(dif, "minus", j, i, start=False, stop=True)
             square((i, j), dif)
+
+        def light_pair(i, j, banks):
+            alone = []
+            for (source, to), bank in zip(((i, j), (j, i)), banks):
+                lone = bank_tile(bank, "alone%d%d" % (source, to))
+                product(lone, "plus", source, to, start=True, stop=True)
+                alone.append(lone)
+            kept = ring.tile([P, D], F32, tag="kept", name="kept%d%d" % (i, j))
+            nc.scalar.copy(out=kept[:], in_=alone[0][:])
+            difference = ring.tile([P, D], F32, tag="difference", name="difference%d%d" % (i, j))
+            nc.vector.tensor_tensor(out=difference[:], in0=alone[1][:], in1=kept[:], op=ALU.subtract)
+            add_to_sum(j, i)
+            park(j, alone[0])
+            square((i, j), difference)
 
         parked = {}
         sum_cols = {}
@@ -267,32 +285,44 @@ def tile_sheaflayer_e_kernel(tc, F, R_words, R_scales, out_0, out_1):
             if j == HALF - 1:
                 park(i, group[i][0])
         park(HALF - 1, group[HALF - 1][0])
-        for j in HIGH:
-            open_sum(j, 4 + (j + 2) % HALF, PATCHES - 1)
+        for j in (4, 5, 6):
+            open_sum(j, 4 + (j + 2) % HALF, PATCHES - 1 - len([pair for pair in LIGHT if pair[1] == j]))
         count = 0
         for i in LOW:
             open_sum(i, 3 * (i % 2), HALF)
-            for j in HIGH:
-                pair_passes(i, j, 1 + count % 2)
+            for j in ORDER:
+                if (i, j) in LIGHT:
+                    light_pair(i, j, (5, 1 + count % 2))
+                else:
+                    pair_passes(i, j, 1 + count % 2)
                 count += 1
                 if j == TURN_AT and i > 0:
                     turn_back(i - 1, 3 * ((i - 1) % 2))
                     finish(i - 1)
             empty(i)
-        for step, (i, j) in enumerate(INSIDE_HIGH):
+        open_sum(7, 5, PATCHES - 1 - HALF)
+        for i, j in INSIDE_HIGH[:-1]:
             pair_passes(i, j, 1 + count % 2)
             count += 1
-            if step == 0:
-                turn_back(3, 3)
-                finish(3)
-            if j == PATCHES - 1 and i < 6:
+            if j == PATCHES - 1:
                 empty(i)
-            if step == 3:
-                turn_back(4, 0)
-                finish(4)
-        for c, bank in ((5, 3), (7, 0), (6, 6)):
+            if (i, j) == (5, 6):
+                for c in (3, 4):
+                    turn_back(c, 3 * (4 - c))
+                for c in (3, 4):
+                    finish(c)
+        i, j = INSIDE_HIGH[-1]
+        dif = bank_tile(1 + count % 2, "dif%d%d" % (i, j))
+        add_to_sum(i, j)
+        product(dif, "plus", i, j, start=True, stop=False)
+        add_to_sum(j, i)
+        empty(j)
+        empty(i)
+        product(dif, "minus", j, i, start=False, stop=True)
+        square((i, j), dif)
+        for c, bank in ((5, 3), (j, 0), (i, 6)):
             turn_back(c, bank)
-        for c in (5, 7, 6):
+        for c in (5, j, i):
             finish(c)
 
         all_rows = psum.tile([P, PAIR_COLUMNS], F32, tag="bank1", name="all_rows")

@@ -29,12 +29,10 @@ LIGHT = [(i, 7) for i in LOW]
 ACROSS = [(i, j) for i in LOW for j in ORDER]
 INSIDE_HIGH = [(i, j) for i in HIGH for j in HIGH if i < j]
 PAIRS = INSIDE_LOW + ACROSS + INSIDE_HIGH
-LAST_ROWS = 4
-LAST_BEHIND = 0
 SYNC_SCALES_AFTER = 24
 PREPARE_AT = 0
 TURN_AT = 5
-LATE_F = 2
+HEAD = ("low", 6, "high", 6, "words", 4, "words",)
 BY_SCALAR = 6
 PAIR_COLUMNS = 32
 
@@ -95,9 +93,6 @@ def tile_sheaflayer_e_kernel(tc, F, R_words, R_scales, out_0, out_1):
                 in_=high_dram[1, j, q].bitcast(dtype),
             )
 
-        load_f(halves[0])
-        for row in range(16 - LAST_ROWS):
-            load_low_scales(row)
         for j in BY_GPSIMD:
             for q in range(4):
                 load_high_scales(nc.gpsimd, F32, j, q)
@@ -109,20 +104,32 @@ def tile_sheaflayer_e_kernel(tc, F, R_words, R_scales, out_0, out_1):
         scales_behind = {}
         for number, (j, q) in enumerate([(j, q) for j in BY_SYNC for q in range(4)]):
             scales_behind[SYNC_SCALES_AFTER + number] = (j, q)
-        for position, (i, j) in enumerate(blocks):
-            if position == LATE_F:
-                load_f(halves[1])
+
+        def load_words():
+            i, j = blocks[len(words)]
             block = keep.tile([P, PACK * D], U8, name="words_%d_%d" % (i, j), align_bytes=64)
             nc.sync.dma_start(
                 out=block[:].bitcast(I32),
                 in_=R_words[PATCHES * i + j].rearrange("p n t -> p (n t)").bitcast(I32),
             )
             words[(i, j)] = block
-            if position == LAST_BEHIND:
-                for row in range(16 - LAST_ROWS, 16):
+            if len(words) in scales_behind:
+                load_high_scales(nc.sync, I32, *scales_behind[len(words)])
+
+        rows = 0
+        for step in HEAD:
+            if step == "low":
+                load_f(halves[0])
+            elif step == "high":
+                load_f(halves[1])
+            elif step == "words":
+                load_words()
+            else:
+                for row in range(rows, rows + step):
                     load_low_scales(row)
-            if position in scales_behind:
-                load_high_scales(nc.sync, I32, *scales_behind[position])
+                rows += step
+        while len(words) < len(blocks):
+            load_words()
 
         grouped = {}
         f_codes = {}
@@ -314,14 +321,15 @@ def tile_sheaflayer_e_kernel(tc, F, R_words, R_scales, out_0, out_1):
         i, j = INSIDE_HIGH[-1]
         dif = bank_tile(1 + count % 2, "dif%d%d" % (i, j))
         add_to_sum(i, j)
-        product(dif, "plus", i, j, start=True, stop=False)
         add_to_sum(j, i)
         empty(j)
         empty(i)
+        turn_back(5, 3)
+        turn_back(j, 0)
+        turn_back(i, 6)
+        product(dif, "plus", i, j, start=True, stop=False)
         product(dif, "minus", j, i, start=False, stop=True)
         square((i, j), dif)
-        for c, bank in ((5, 3), (j, 0), (i, 6)):
-            turn_back(c, bank)
         for c in (5, j, i):
             finish(c)
 
@@ -335,4 +343,4 @@ def tile_sheaflayer_e_kernel(tc, F, R_words, R_scales, out_0, out_1):
         loss_cell = out_1
         for step in range(2 - out_1.ndim):
             loss_cell = loss_cell.unsqueeze(0)
-        nc.sync.dma_start(out=loss_cell, in_=loss[0:1, :])
+        nc.scalar.dma_start(out=loss_cell, in_=loss[0:1, :])

from contextlib import ExitStack

import concourse.mybir as mybir
from concourse.masks import make_identity

F32 = mybir.dt.float32
BF16 = mybir.dt.bfloat16
I32 = mybir.dt.int32
U32 = mybir.dt.uint32
U8 = mybir.dt.uint8
FP8X4 = mybir.dt.float8_e4m3fn_x4
ALU = mybir.AluOpType
ACT = mybir.ActivationFunctionType

P = 128
PACK = 4
PATCHES = 8
D = 512
B = 128
PLANES = 4
HALF = PATCHES // 2
BY_GPSIMD = (0, 1, 2, 3, 4)
BY_SYNC = (5, 6, 7)
LOW = list(range(HALF))
HIGH = list(range(HALF, PATCHES))
INSIDE_LOW = [(i, j) for i in LOW for j in LOW if i < j]
ORDER = (4, 5, 7, 6)
LIGHT = [(i, 7) for i in LOW]
ACROSS = [(i, j) for i in LOW for j in ORDER]
INSIDE_HIGH = [(i, j) for i in HIGH for j in HIGH if i < j]
PAIRS = INSIDE_LOW + ACROSS + INSIDE_HIGH
SYNC_SCALES_AFTER = 24
PREPARE_AT = 0
TURN_AT = 5
HEAD = ("low", 6, "high", 6, "words", 4, "words",)
BY_SCALAR = 6
PAIR_COLUMNS = 32

FLOPS = 2 * (2 * PATCHES * (PATCHES - 1) * D * D * B)
BYTES = (
    PATCHES * D * B * 2
    + PATCHES * (PATCHES - 1) * (D * D + D * D // 32)
    + PATCHES * D * B * 4
    + 4
)


def tile_sheaflayer_e_kernel(tc, F, R_words, R_scales, out_0, out_1):
    nc = tc.nc
    with ExitStack() as ctx:
        keep = ctx.enter_context(tc.tile_pool(name="keep", bufs=1))
        ring = ctx.enter_context(tc.tile_pool(name="ring", bufs=4))
        psum = ctx.enter_context(tc.psum_pool(name="psum", bufs=1))
        ctx.enter_context(tc.manual_schedule())

        low_planes = keep.tile([P, PATCHES, D], U8, align_bytes=64)
        nc.vector.memset(low_planes[:].bitcast(I32), 0)
        high_planes = []
        for j in range(PATCHES):
            plane_tile = keep.tile([P, D], U8, name="high_planes%d" % j, align_bytes=64)
            nc.vector.memset(plane_tile[:].bitcast(I32), 0)
            high_planes.append(plane_tile)
        pair_sums = keep.tile([P, PAIR_COLUMNS], F32)
        nc.vector.memset(pair_sums[:], 0.0)
        ones = keep.tile([P, P], F32)
        nc.vector.memset(ones[:], 1.0)

        f_rows = keep.tile([P, PATCHES, PACK, B], BF16)
        f_dram = F.rearrange("i (p t) b -> p i (t b)", t=PACK)
        halves = [slice(0, HALF), slice(HALF, PATCHES)]

        def load_f(half):
            nc.sync.dma_start(
                out=f_rows[:, half].rearrange("p i t b -> p i (t b)"), in_=f_dram[:, half]
            )

        identity = keep.tile([P, P], F32)
        make_identity(nc, identity[:])

        low_dram = R_scales.rearrange("(h o j) (q r) n -> h q r o j n", h=2, o=PLANES, r=4)
        high_dram = R_scales.rearrange("(h o j) (q r) n -> h j q o r n", h=2, o=PLANES, r=4)

        def load_low_scales(row):
            q, r = row // 4, row % 4
            nc.sync.dma_start(
                out=low_planes[32 * q + r : 32 * q + 4 * PLANES : 4].bitcast(I32),
                in_=low_dram[0, q, r].bitcast(I32),
            )

        def load_high_scales(queue, dtype, j, q):
            queue.dma_start(
                out=high_planes[j][32 * q : 32 * q + 4 * PLANES].bitcast(dtype),
                in_=high_dram[1, j, q].bitcast(dtype),
            )

        for j in BY_GPSIMD:
            for q in range(4):
                load_high_scales(nc.gpsimd, F32, j, q)

        words = {}
        blocks = []
        for i, j in PAIRS:
            blocks += [(i, j), (j, i)]
        scales_behind = {}
        for number, (j, q) in enumerate([(j, q) for j in BY_SYNC for q in range(4)]):
            scales_behind[SYNC_SCALES_AFTER + number] = (j, q)

        def load_words():
            i, j = blocks[len(words)]
            block = keep.tile([P, PACK * D], U8, name="words_%d_%d" % (i, j), align_bytes=64)
            nc.sync.dma_start(
                out=block[:].bitcast(I32),
                in_=R_words[PATCHES * i + j].rearrange("p n t -> p (n t)").bitcast(I32),
            )
            words[(i, j)] = block
            if len(words) in scales_behind:
                load_high_scales(nc.sync, I32, *scales_behind[len(words)])

        rows = 0
        for step in HEAD:
            if step == "low":
                load_f(halves[0])
            elif step == "high":
                load_f(halves[1])
            elif step == "words":
                load_words()
            else:
                for row in range(rows, rows + step):
                    load_low_scales(row)
                rows += step
        while len(words) < len(blocks):
            load_words()

        grouped = {}
        f_codes = {}
        f_scales = {}
        for sign in ("plus", "minus"):
            grouped[sign] = keep.tile(
                [P, PATCHES, B, PACK], BF16, name="grouped_" + sign, align_bytes=64
            )
            f_codes[sign] = keep.tile([P, PATCHES, B], U32, name="f_codes_" + sign, align_bytes=64)
            f_scales[sign] = keep.tile([P, PATCHES, B], U8, name="f_scales_" + sign, align_bytes=64)

        def regroup(sign, four):
            by_column = f_rows[:, four].rearrange("p i t b -> p i b t")
            if sign == "plus":
                nc.vector.tensor_copy(out=grouped[sign][:, four], in_=by_column)
            else:
                nc.scalar.mul(out=grouped[sign][:, four], in_=by_column, mul=-1.0)

        def quantise(sign, four):
            nc.vector.quantize_mx(
                out=f_codes[sign][:, four].rearrange("p i b -> p (i b)").bitcast(FP8X4),
                scales=f_scales[sign][:, four].rearrange("p i b -> p (i b)"),
                in_=grouped[sign][:, four].rearrange("p i b t -> p (i b t)"),
            )

        def prepare(four):
            regroup("plus", four)
            regroup("minus", four)
            quantise("plus", four)
            quantise("minus", four)

        prepare(halves[0])

        group = {}

        def bank_tile(bank, name):
            return psum.tile([P, D], F32, tag="bank%d" % bank, name=name)

        def plane(i, j):
            if i < HALF:
                return low_planes[4 * i : P, j, :]
            return high_planes[j][4 * (i % HALF) : P, :]

        def product(bank, sign, i, j, start, stop):
            nc.tensor.matmul_mx(
                out=bank[:],
                lhsT=f_codes[sign][:, i, :].bitcast(FP8X4),
                lhsT_scale=f_scales[sign][:, i, :],
                rhs=words[(i, j)][:].bitcast(FP8X4),
                rhs_scale=plane(i, j),
                start=start,
                stop=stop,
            )

        def open_sum(j, bank, passes):
            group[j] = [bank_tile(bank, "sum%d_of_%d" % (j, passes)), 0, passes]

        def add_to_sum(i, j):
            bank, done, passes = group[j]
            product(bank, "plus", i, j, start=(done == 0), stop=(done == passes - 1))
            group[j][1] = done + 1

        def square(pair, dif):
            index = PAIRS.index(pair)
            squares = ring.tile([P, D], F32, tag="squares", name="squares%d" % index)
            nc.scalar.activation(
                out=squares[:],
                in_=dif[:],
                func=ACT.Square,
                accum_out=pair_sums[:, index : index + 1],
            )

        def pair_passes(i, j, dif_bank):
            dif = bank_tile(dif_bank, "dif%d%d" % (i, j))
            add_to_sum(i, j)
            product(dif, "plus", i, j, start=True, stop=False)
            add_to_sum(j, i)
            product(dif, "minus", j, i, start=False, stop=True)
            square((i, j), dif)

        def light_pair(i, j, banks):
            alone = []
            for (source, to), bank in zip(((i, j), (j, i)), banks):
                lone = bank_tile(bank, "alone%d%d" % (source, to))
                product(lone, "plus", source, to, start=True, stop=True)
                alone.append(lone)
            kept = ring.tile([P, D], F32, tag="kept", name="kept%d%d" % (i, j))
            nc.scalar.copy(out=kept[:], in_=alone[0][:])
            difference = ring.tile([P, D], F32, tag="difference", name="difference%d%d" % (i, j))
            nc.vector.tensor_tensor(out=difference[:], in0=alone[1][:], in1=kept[:], op=ALU.subtract)
            add_to_sum(j, i)
            park(j, alone[0])
            square((i, j), difference)

        parked = {}
        sum_cols = {}

        def empty(j):
            by_t = group[j][0][:].rearrange("b (m t) -> b t m", t=PACK)
            cols = ring.tile([P, PACK, P], F32, tag="sum_cols", name="sum_cols%d" % j)
            if j in parked:
                nc.vector.scalar_tensor_tensor(
                    out=cols[:],
                    in0=by_t,
                    scalar=1.0 / PATCHES,
                    in1=parked[j][:],
                    op0=ALU.mult,
                    op1=ALU.add,
                )
            elif j == BY_SCALAR:
                nc.scalar.mul(out=cols[:], in_=by_t, mul=1.0 / PATCHES)
            else:
                nc.vector.tensor_scalar_mul(out=cols[:], in0=by_t, scalar1=1.0 / PATCHES)
            sum_cols[j] = cols

        def park(j, block):
            by_t = block[:].rearrange("b (m t) -> b t m", t=PACK)
            if j not in parked:
                parked[j] = keep.tile([P, PACK, P], F32, name="parked%d" % j)
                nc.vector.tensor_scalar_mul(out=parked[j][:], in0=by_t, scalar1=1.0 / PATCHES)
            else:
                nc.vector.scalar_tensor_tensor(
                    out=parked[j][:],
                    in0=by_t,
                    scalar=1.0 / PATCHES,
                    in1=parked[j][:],
                    op0=ALU.mult,
                    op1=ALU.add,
                )

        backs = {}

        def turn_back(j, bank):
            back = psum.tile([P, PACK, B], F32, tag="bank%d" % bank, name="back%d" % j)
            for t in range(PACK):
                nc.tensor.transpose(back[:, t, :], sum_cols[j][:, t, :], identity[:])
            backs[j] = back

        def finish(j):
            updated = keep.tile([P, PACK, B], F32, name="updated%d" % j)
            nc.vector.scalar_tensor_tensor(
                out=updated[:],
                in0=f_rows[:, j],
                scalar=1.0 / PATCHES,
                in1=backs[j][:],
                op0=ALU.mult,
                op1=ALU.add,
            )
            nc.sync.dma_start(
                out=out_0[j].rearrange("(m t) b -> m (t b)", t=PACK),
                in_=updated[:].rearrange("m t b -> m (t b)"),
            )

        for j in LOW:
            open_sum(j, j, HALF - 1)
        for step, (i, j) in enumerate(INSIDE_LOW):
            pair_passes(i, j, 4 + step % 4)
            if step == PREPARE_AT:
                prepare(halves[1])
            if j == HALF - 1:
                park(i, group[i][0])
        park(HALF - 1, group[HALF - 1][0])
        for j in (4, 5, 6):
            open_sum(j, 4 + (j + 2) % HALF, PATCHES - 1 - len([pair for pair in LIGHT if pair[1] == j]))
        count = 0
        for i in LOW:
            open_sum(i, 3 * (i % 2), HALF)
            for j in ORDER:
                if (i, j) in LIGHT:
                    light_pair(i, j, (5, 1 + count % 2))
                else:
                    pair_passes(i, j, 1 + count % 2)
                count += 1
                if j == TURN_AT and i > 0:
                    turn_back(i - 1, 3 * ((i - 1) % 2))
                    finish(i - 1)
            empty(i)
        open_sum(7, 5, PATCHES - 1 - HALF)
        for i, j in INSIDE_HIGH[:-1]:
            pair_passes(i, j, 1 + count % 2)
            count += 1
            if j == PATCHES - 1:
                empty(i)
            if (i, j) == (5, 6):
                for c in (3, 4):
                    turn_back(c, 3 * (4 - c))
                for c in (3, 4):
                    finish(c)
        i, j = INSIDE_HIGH[-1]
        dif = bank_tile(1 + count % 2, "dif%d%d" % (i, j))
        add_to_sum(i, j)
        add_to_sum(j, i)
        empty(j)
        empty(i)
        turn_back(5, 3)
        turn_back(j, 0)
        turn_back(i, 6)
        product(dif, "plus", i, j, start=True, stop=False)
        product(dif, "minus", j, i, start=False, stop=True)
        square((i, j), dif)
        for c in (5, j, i):
            finish(c)

        all_rows = psum.tile([P, PAIR_COLUMNS], F32, tag="bank1", name="all_rows")
        nc.tensor.matmul(out=all_rows[:], lhsT=ones[:], rhs=pair_sums[:], start=True, stop=True)
        scaled = keep.tile([P, PAIR_COLUMNS], F32)
        loss = keep.tile([P, 1], F32)
        nc.scalar.activation(
            out=scaled[:], in_=all_rows[:], func=ACT.Copy, scale=0.1, accum_out=loss[:]
        )
        loss_cell = out_1
        for step in range(2 - out_1.ndim):
            loss_cell = loss_cell.unsqueeze(0)
        nc.scalar.dma_start(out=loss_cell, in_=loss[0:1, :])
